import numpy as np
import ml_dtypes

BF16 = ml_dtypes.bfloat16


def bf(x):
    return np.asarray(x, np.float32).astype(BF16)


def f32(x):
    return np.asarray(x, np.float32)


def f64(x):
    return np.asarray(x).astype(np.float64)


def striped(idx):
    return np.tile(idx.reshape(-1, 16).T, (8, 1))


C, S, N = 256, 4096, 2048
BASE = 10000.0


def make_pe():
    pos = np.arange(1, N + 1, dtype=np.float64)[None, :]
    div = np.exp(np.arange(0, C, 2, dtype=np.float64) * (-np.log(BASE) / C))[:, None]
    pe = np.zeros((C, N))
    pe[0::2] = np.sin(div * pos)
    pe[1::2] = np.cos(div * pos)
    return pe


def setup_inputs():
    return {"tok_emb": f32(np.random.standard_normal((C, S))), "pe": f32(make_pe()), "offs": striped(np.random.permutation(np.tile(np.arange(S), 2))[:N])}


def reference(tok_emb, pe, offs):
    idx = offs[:16].T.reshape(-1)
    return f64(tok_emb)[:, idx] + f64(pe)

@@ -1,0 +1,26 @@
+import concourse.mybir as mybir
+
+P = 128
+F32 = mybir.dt.float32
+U16 = mybir.dt.uint16
+ADD = mybir.AluOpType.add
+
+
+def tile_transformerlayer_kernel(tc, tok_emb, pe, offs, out):
+    nc = tc.nc
+    channels, words = tok_emb.shape
+    places = pe.shape[1]
+
+    with tc.tile_pool(name="held", bufs=1) as held:
+        offsets = held.tile([P, places // 16], U16, name="offsets")
+        nc.sync.dma_start(offsets[:], offs)
+
+        for b in range(channels // P):
+            rows = slice(b * P, (b + 1) * P)
+            table = held.tile([P, words], F32, name=f"table{b}")
+            position = held.tile([P, places], F32, name=f"position{b}")
+            summed = held.tile([P, places], F32, name=f"summed{b}")
+            nc.sync.dma_start(table[:], tok_emb[rows, :])
+            nc.scalar.dma_start(position[:], pe[rows, :])
+            nc.vector.tensor_tensor(summed[:], table[:].indirect(offsets[:]), position[:], ADD)
+            nc.sync.dma_start(out[rows, :], summed[:])

@@ -1,6 +1,7 @@
 import concourse.mybir as mybir
 
 P = 128
+PIECE = 512
 F32 = mybir.dt.float32
 U16 = mybir.dt.uint16
 ADD = mybir.AluOpType.add
@@ -10,17 +11,28 @@ def tile_transformerlayer_kernel(tc, tok_emb, pe, offs, out):
     nc = tc.nc
     channels, words = tok_emb.shape
     places = pe.shape[1]
+    blocks = range(channels // P)
+    pieces = range(places // PIECE)
 
     with tc.tile_pool(name="held", bufs=1) as held:
         offsets = held.tile([P, places // 16], U16, name="offsets")
         nc.sync.dma_start(offsets[:], offs)
 
-        for b in range(channels // P):
+        tables = [held.tile([P, words], F32, name=f"table{b}") for b in blocks]
+        positions = [held.tile([P, places], F32, name=f"position{b}") for b in blocks]
+        sums = [held.tile([P, places], F32, name=f"summed{b}") for b in blocks]
+
+        for b in blocks:
             rows = slice(b * P, (b + 1) * P)
-            table = held.tile([P, words], F32, name=f"table{b}")
-            position = held.tile([P, places], F32, name=f"position{b}")
-            summed = held.tile([P, places], F32, name=f"summed{b}")
-            nc.sync.dma_start(table[:], tok_emb[rows, :])
-            nc.scalar.dma_start(position[:], pe[rows, :])
-            nc.vector.tensor_tensor(summed[:], table[:].indirect(offsets[:]), position[:], ADD)
-            nc.sync.dma_start(out[rows, :], summed[:])
+            nc.sync.dma_start(tables[b][:], tok_emb[rows, :])
+            for k in pieces:
+                cols = slice(k * PIECE, (k + 1) * PIECE)
+                nc.sync.dma_start(positions[b][:, cols], pe[rows, cols])
+
+        for b in blocks:
+            rows = slice(b * P, (b + 1) * P)
+            for k in pieces:
+                cols = slice(k * PIECE, (k + 1) * PIECE)
+                picked = tables[b][:].indirect(offsets[:, k * (PIECE // 16) : (k + 1) * (PIECE // 16)])
+                nc.vector.tensor_tensor(sums[b][:, cols], picked, positions[b][:, cols], ADD)
+                nc.sync.dma_start(out[rows, cols], sums[b][:, cols])

@@ -1,7 +1,7 @@
 import concourse.mybir as mybir
 
 P = 128
-PIECE = 512
+PIECE = (1024, 512)
 F32 = mybir.dt.float32
 U16 = mybir.dt.uint16
 ADD = mybir.AluOpType.add
@@ -12,7 +12,6 @@ def tile_transformerlayer_kernel(tc, tok_emb, pe, offs, out):
     channels, words = tok_emb.shape
     places = pe.shape[1]
     blocks = range(channels // P)
-    pieces = range(places // PIECE)
 
     with tc.tile_pool(name="held", bufs=1) as held:
         offsets = held.tile([P, places // 16], U16, name="offsets")
@@ -25,14 +24,14 @@ def tile_transformerlayer_kernel(tc, tok_emb, pe, offs, out):
         for b in blocks:
             rows = slice(b * P, (b + 1) * P)
             nc.sync.dma_start(tables[b][:], tok_emb[rows, :])
-            for k in pieces:
-                cols = slice(k * PIECE, (k + 1) * PIECE)
+            for start in range(0, places, PIECE[b]):
+                cols = slice(start, start + PIECE[b])
                 nc.sync.dma_start(positions[b][:, cols], pe[rows, cols])
 
         for b in blocks:
             rows = slice(b * P, (b + 1) * P)
-            for k in pieces:
-                cols = slice(k * PIECE, (k + 1) * PIECE)
-                picked = tables[b][:].indirect(offsets[:, k * (PIECE // 16) : (k + 1) * (PIECE // 16)])
+            for start in range(0, places, PIECE[b]):
+                cols = slice(start, start + PIECE[b])
+                picked = tables[b][:].indirect(offsets[:, start // 16 : (start + PIECE[b]) // 16])
                 nc.vector.tensor_tensor(sums[b][:, cols], picked, positions[b][:, cols], ADD)
                 nc.sync.dma_start(out[rows, cols], sums[b][:, cols])

@@ -1,7 +1,7 @@
 import concourse.mybir as mybir
 
 P = 128
-PIECE = (1024, 512)
+PIECES = ((1024, 1024), (256, 512, 512, 512, 256))
 F32 = mybir.dt.float32
 U16 = mybir.dt.uint16
 ADD = mybir.AluOpType.add
@@ -12,6 +12,7 @@ def tile_transformerlayer_kernel(tc, tok_emb, pe, offs, out):
     channels, words = tok_emb.shape
     places = pe.shape[1]
     blocks = range(channels // P)
+    bounds = [[(sum(widths[:k]), sum(widths[: k + 1])) for k in range(len(widths))] for widths in PIECES]
 
     with tc.tile_pool(name="held", bufs=1) as held:
         offsets = held.tile([P, places // 16], U16, name="offsets")
@@ -24,14 +25,12 @@ def tile_transformerlayer_kernel(tc, tok_emb, pe, offs, out):
         for b in blocks:
             rows = slice(b * P, (b + 1) * P)
             nc.sync.dma_start(tables[b][:], tok_emb[rows, :])
-            for start in range(0, places, PIECE[b]):
-                cols = slice(start, start + PIECE[b])
-                nc.sync.dma_start(positions[b][:, cols], pe[rows, cols])
+            for first, end in bounds[b]:
+                nc.sync.dma_start(positions[b][:, first:end], pe[rows, first:end])
 
         for b in blocks:
             rows = slice(b * P, (b + 1) * P)
-            for start in range(0, places, PIECE[b]):
-                cols = slice(start, start + PIECE[b])
-                picked = tables[b][:].indirect(offsets[:, start // 16 : (start + PIECE[b]) // 16])
-                nc.vector.tensor_tensor(sums[b][:, cols], picked, positions[b][:, cols], ADD)
-                nc.sync.dma_start(out[rows, cols], sums[b][:, cols])
+            for first, end in bounds[b]:
+                picked = tables[b][:].indirect(offsets[:, first // 16 : end // 16])
+                nc.vector.tensor_tensor(sums[b][:, first:end], picked, positions[b][:, first:end], ADD)
+                nc.sync.dma_start(out[rows, first:end], sums[b][:, first:end])

@@ -1,10 +1,16 @@
 import concourse.mybir as mybir
 
 P = 128
-PIECES = ((1024, 1024), (256, 512, 512, 512, 256))
+ADDS = ((1024, 1024), (256, 512, 512, 512, 256))
+LOADS = ((1024, 1024), (256, 512, 1280))
+STORES = ((2048,), (1280, 512, 256))
 F32 = mybir.dt.float32
 U16 = mybir.dt.uint16
 ADD = mybir.AluOpType.add
+
+
+def cuts(widths):
+    return [(sum(widths[:k]), sum(widths[: k + 1])) for k in range(len(widths))]
 
 
 def tile_transformerlayer_kernel(tc, tok_emb, pe, offs, out):
@@ -12,7 +18,6 @@ def tile_transformerlayer_kernel(tc, tok_emb, pe, offs, out):
     channels, words = tok_emb.shape
     places = pe.shape[1]
     blocks = range(channels // P)
-    bounds = [[(sum(widths[:k]), sum(widths[: k + 1])) for k in range(len(widths))] for widths in PIECES]
 
     with tc.tile_pool(name="held", bufs=1) as held:
         offsets = held.tile([P, places // 16], U16, name="offsets")
@@ -25,12 +30,14 @@ def tile_transformerlayer_kernel(tc, tok_emb, pe, offs, out):
         for b in blocks:
             rows = slice(b * P, (b + 1) * P)
             nc.sync.dma_start(tables[b][:], tok_emb[rows, :])
-            for first, end in bounds[b]:
+            for first, end in cuts(LOADS[b]):
                 nc.sync.dma_start(positions[b][:, first:end], pe[rows, first:end])
 
         for b in blocks:
             rows = slice(b * P, (b + 1) * P)
-            for first, end in bounds[b]:
+            for first, end in cuts(ADDS[b]):
                 picked = tables[b][:].indirect(offsets[:, first // 16 : end // 16])
                 nc.vector.tensor_tensor(sums[b][:, first:end], picked, positions[b][:, first:end], ADD)
-                nc.sync.dma_start(out[rows, first:end], sums[b][:, first:end])
+                for store_first, store_end in cuts(STORES[b]):
+                    if store_end == end:
+                        nc.sync.dma_start(out[rows, store_first:store_end], sums[b][:, store_first:store_end])

@@ -1,9 +1,9 @@
 import concourse.mybir as mybir
 
 P = 128
-ADDS = ((1024, 1024), (256, 512, 512, 512, 256))
-LOADS = ((1024, 1024), (256, 512, 1280))
-STORES = ((2048,), (1280, 512, 256))
+ADDS = ((1024, 1024), (256, 256, 512, 512, 256, 256))
+LOADS = ((1024, 1024), (256, 256, 512, 1024))
+STORES = ((2048,), (1024, 512, 256, 256))
 F32 = mybir.dt.float32
 U16 = mybir.dt.uint16
 ADD = mybir.AluOpType.add

@@ -1,9 +1,9 @@
 import concourse.mybir as mybir
 
 P = 128
-ADDS = ((1024, 1024), (256, 256, 512, 512, 256, 256))
-LOADS = ((1024, 1024), (256, 256, 512, 1024))
-STORES = ((2048,), (1024, 512, 256, 256))
+ADDS = ((1024, 1024), (128, 128, 256, 512, 512, 256, 128, 128))
+LOADS = ((1024, 1024), (128, 128, 256, 512, 1024))
+STORES = ((2048,), (1024, 512, 256, 128, 128))
 F32 = mybir.dt.float32
 U16 = mybir.dt.uint16
 ADD = mybir.AluOpType.add

@@ -29,9 +29,10 @@ def tile_transformerlayer_kernel(tc, tok_emb, pe, offs, out):
 
         for b in blocks:
             rows = slice(b * P, (b + 1) * P)
-            nc.sync.dma_start(tables[b][:], tok_emb[rows, :])
-            for first, end in cuts(LOADS[b]):
+            for k, (first, end) in enumerate(cuts(LOADS[b])):
                 nc.sync.dma_start(positions[b][:, first:end], pe[rows, first:end])
+                if k == 0:
+                    nc.sync.dma_start(tables[b][:], tok_emb[rows, :])
 
         for b in blocks:
             rows = slice(b * P, (b + 1) * P)

@@ -4,6 +4,7 @@ P = 128
 ADDS = ((1024, 1024), (128, 128, 256, 512, 512, 256, 128, 128))
 LOADS = ((1024, 1024), (128, 128, 256, 512, 1024))
 STORES = ((2048,), (1024, 512, 256, 128, 128))
+ALIGN = 4096
 F32 = mybir.dt.float32
 U16 = mybir.dt.uint16
 ADD = mybir.AluOpType.add
@@ -23,9 +24,9 @@ def tile_transformerlayer_kernel(tc, tok_emb, pe, offs, out):
         offsets = held.tile([P, places // 16], U16, name="offsets")
         nc.sync.dma_start(offsets[:], offs)
 
-        tables = [held.tile([P, words], F32, name=f"table{b}") for b in blocks]
-        positions = [held.tile([P, places], F32, name=f"position{b}") for b in blocks]
-        sums = [held.tile([P, places], F32, name=f"summed{b}") for b in blocks]
+        tables = [held.tile([P, words], F32, name=f"table{b}", align_bytes=ALIGN) for b in blocks]
+        positions = [held.tile([P, places], F32, name=f"position{b}", align_bytes=ALIGN) for b in blocks]
+        sums = [held.tile([P, places], F32, name=f"summed{b}", align_bytes=ALIGN) for b in blocks]
 
         for b in blocks:
             rows = slice(b * P, (b + 1) * P)

@@ -21,7 +21,7 @@ def tile_transformerlayer_kernel(tc, tok_emb, pe, offs, out):
     blocks = range(channels // P)
 
     with tc.tile_pool(name="held", bufs=1) as held:
-        offsets = held.tile([P, places // 16], U16, name="offsets")
+        offsets = held.tile([P, places // 16], U16, name="offsets", align_bytes=ALIGN)
         nc.sync.dma_start(offsets[:], offs)
 
         tables = [held.tile([P, words], F32, name=f"table{b}", align_bytes=ALIGN) for b in blocks]

@@ -22,18 +22,18 @@ def tile_transformerlayer_kernel(tc, tok_emb, pe, offs, out):
 
     with tc.tile_pool(name="held", bufs=1) as held:
         offsets = held.tile([P, places // 16], U16, name="offsets", align_bytes=ALIGN)
-        nc.sync.dma_start(offsets[:], offs)
-
         tables = [held.tile([P, words], F32, name=f"table{b}", align_bytes=ALIGN) for b in blocks]
         positions = [held.tile([P, places], F32, name=f"position{b}", align_bytes=ALIGN) for b in blocks]
         sums = [held.tile([P, places], F32, name=f"summed{b}", align_bytes=ALIGN) for b in blocks]
 
+        nc.sync.dma_start(tables[0][:], tok_emb[:P, :])
+        nc.sync.dma_start(offsets[:], offs)
         for b in blocks:
             rows = slice(b * P, (b + 1) * P)
             for k, (first, end) in enumerate(cuts(LOADS[b])):
                 nc.sync.dma_start(positions[b][:, first:end], pe[rows, first:end])
-                if k == 0:
-                    nc.sync.dma_start(tables[b][:], tok_emb[rows, :])
+                if b == 1 and k == 0:
+                    nc.sync.dma_start(tables[1][:], tok_emb[rows, :])
 
         for b in blocks:
             rows = slice(b * P, (b + 1) * P)

@@ -2,7 +2,7 @@ import concourse.mybir as mybir
 
 P = 128
 ADDS = ((1024, 1024), (128, 128, 256, 512, 512, 256, 128, 128))
-LOADS = ((1024, 1024), (128, 128, 256, 512, 1024))
+LOADS = ((128, 896, 1024), (128, 128, 256, 512, 1024))
 STORES = ((2048,), (1024, 512, 256, 128, 128))
 ALIGN = 4096
 F32 = mybir.dt.float32
@@ -23,23 +23,25 @@ def tile_transformerlayer_kernel(tc, tok_emb, pe, offs, out):
     with tc.tile_pool(name="held", bufs=1) as held:
         offsets = held.tile([P, places // 16], U16, name="offsets", align_bytes=ALIGN)
         tables = [held.tile([P, words], F32, name=f"table{b}", align_bytes=ALIGN) for b in blocks]
-        positions = [held.tile([P, places], F32, name=f"position{b}", align_bytes=ALIGN) for b in blocks]
+        positions = held.tile([P, len(blocks), places], F32, name="positions", align_bytes=ALIGN)
         sums = [held.tile([P, places], F32, name=f"summed{b}", align_bytes=ALIGN) for b in blocks]
 
         nc.sync.dma_start(tables[0][:], tok_emb[:P, :])
         nc.sync.dma_start(offsets[:], offs)
+        piece = LOADS[0][0]
+        nc.sync.dma_start(positions[:, :, :piece], pe.rearrange("(b p) n -> p b n", p=P)[:, :, :piece])
         for b in blocks:
             rows = slice(b * P, (b + 1) * P)
-            for k, (first, end) in enumerate(cuts(LOADS[b])):
-                nc.sync.dma_start(positions[b][:, first:end], pe[rows, first:end])
-                if b == 1 and k == 0:
-                    nc.sync.dma_start(tables[1][:], tok_emb[rows, :])
+            if b == 1:
+                nc.sync.dma_start(tables[1][:], tok_emb[rows, :])
+            for first, end in cuts(LOADS[b])[1:]:
+                nc.sync.dma_start(positions[:, b, first:end], pe[rows, first:end])
 
         for b in blocks:
             rows = slice(b * P, (b + 1) * P)
             for first, end in cuts(ADDS[b]):
                 picked = tables[b][:].indirect(offsets[:, first // 16 : end // 16])
-                nc.vector.tensor_tensor(sums[b][:, first:end], picked, positions[b][:, first:end], ADD)
+                nc.vector.tensor_tensor(sums[b][:, first:end], picked, positions[:, b, first:end], ADD)
                 for store_first, store_end in cuts(STORES[b]):
                     if store_end == end:
                         nc.sync.dma_start(out[rows, store_first:store_end], sums[b][:, store_first:store_end])

@@ -1,9 +1,9 @@
 import concourse.mybir as mybir
 
 P = 128
-ADDS = ((1024, 1024), (128, 128, 256, 512, 512, 256, 128, 128))
-LOADS = ((128, 896, 1024), (128, 128, 256, 512, 1024))
-STORES = ((2048,), (1024, 512, 256, 128, 128))
+ADDS = (1024, 1024, 128, 128, 256, 512, 512, 256, 128, 128)
+LOADS = (1024, 896, 256, 128, 256, 512, 1024)
+STORES = (2048, 1024, 512, 256, 128, 128)
 ALIGN = 4096
 F32 = mybir.dt.float32
 U16 = mybir.dt.uint16
@@ -16,32 +16,29 @@ def cuts(widths):
 
 def tile_transformerlayer_kernel(tc, tok_emb, pe, offs, out):
     nc = tc.nc
-    channels, words = tok_emb.shape
+    words = tok_emb.shape[1]
     places = pe.shape[1]
-    blocks = range(channels // P)
+    table_rows = tok_emb.rearrange("(p b) w -> p b w", p=P)
+    pe_rows = pe.rearrange("(p b) n -> p (b n)", p=P)
+    out_rows = out.rearrange("(p b) n -> p (b n)", p=P)
 
     with tc.tile_pool(name="held", bufs=1) as held:
         offsets = held.tile([P, places // 16], U16, name="offsets", align_bytes=ALIGN)
-        tables = [held.tile([P, words], F32, name=f"table{b}", align_bytes=ALIGN) for b in blocks]
-        positions = held.tile([P, len(blocks), places], F32, name="positions", align_bytes=ALIGN)
-        sums = [held.tile([P, places], F32, name=f"summed{b}", align_bytes=ALIGN) for b in blocks]
+        tables = [held.tile([P, words], F32, name=f"table{b}", align_bytes=ALIGN) for b in range(2)]
+        positions = held.tile([P, 2 * places], F32, name="positions", align_bytes=ALIGN)
+        sums = held.tile([P, 2 * places], F32, name="sums", align_bytes=ALIGN)
 
-        nc.sync.dma_start(tables[0][:], tok_emb[:P, :])
+        nc.sync.dma_start(tables[0][:], table_rows[:, 0, :])
         nc.sync.dma_start(offsets[:], offs)
-        piece = LOADS[0][0]
-        nc.sync.dma_start(positions[:, :, :piece], pe.rearrange("(b p) n -> p b n", p=P)[:, :, :piece])
-        for b in blocks:
-            rows = slice(b * P, (b + 1) * P)
-            if b == 1:
-                nc.sync.dma_start(tables[1][:], tok_emb[rows, :])
-            for first, end in cuts(LOADS[b])[1:]:
-                nc.sync.dma_start(positions[:, b, first:end], pe[rows, first:end])
+        for first, end in cuts(LOADS):
+            nc.sync.dma_start(positions[:, first:end], pe_rows[:, first:end])
+            if first < places < end:
+                nc.sync.dma_start(tables[1][:], table_rows[:, 1, :])
 
-        for b in blocks:
-            rows = slice(b * P, (b + 1) * P)
-            for first, end in cuts(ADDS[b]):
-                picked = tables[b][:].indirect(offsets[:, first // 16 : end // 16])
-                nc.vector.tensor_tensor(sums[b][:, first:end], picked, positions[:, b, first:end], ADD)
-                for store_first, store_end in cuts(STORES[b]):
-                    if store_end == end:
-                        nc.sync.dma_start(out[rows, store_first:store_end], sums[b][:, store_first:store_end])
+        for first, end in cuts(ADDS):
+            b = first // places
+            picked = tables[b][:].indirect(offsets[:, (first - b * places) // 16 : (end - b * places) // 16])
+            nc.vector.tensor_tensor(sums[:, first:end], picked, positions[:, first:end], ADD)
+            for store_first, store_end in cuts(STORES):
+                if store_end == end:
+                    nc.sync.dma_start(out_rows[:, store_first:store_end], sums[:, store_first:store_end])

import concourse.mybir as mybir

P = 128
ADDS = (1024, 1024, 128, 128, 256, 512, 512, 256, 128, 128)
LOADS = (1024, 896, 256, 128, 256, 512, 1024)
STORES = (2048, 1024, 512, 256, 128, 128)
ALIGN = 4096
F32 = mybir.dt.float32
U16 = mybir.dt.uint16
ADD = mybir.AluOpType.add


def cuts(widths):
    return [(sum(widths[:k]), sum(widths[: k + 1])) for k in range(len(widths))]


def tile_transformerlayer_kernel(tc, tok_emb, pe, offs, out):
    nc = tc.nc
    words = tok_emb.shape[1]
    places = pe.shape[1]
    table_rows = tok_emb.rearrange("(p b) w -> p b w", p=P)
    pe_rows = pe.rearrange("(p b) n -> p (b n)", p=P)
    out_rows = out.rearrange("(p b) n -> p (b n)", p=P)

    with tc.tile_pool(name="held", bufs=1) as held:
        offsets = held.tile([P, places // 16], U16, name="offsets", align_bytes=ALIGN)
        tables = [held.tile([P, words], F32, name=f"table{b}", align_bytes=ALIGN) for b in range(2)]
        positions = held.tile([P, 2 * places], F32, name="positions", align_bytes=ALIGN)
        sums = held.tile([P, 2 * places], F32, name="sums", align_bytes=ALIGN)

        nc.sync.dma_start(tables[0][:], table_rows[:, 0, :])
        nc.sync.dma_start(offsets[:], offs)
        for first, end in cuts(LOADS):
            nc.sync.dma_start(positions[:, first:end], pe_rows[:, first:end])
            if first < places < end:
                nc.sync.dma_start(tables[1][:], table_rows[:, 1, :])

        for first, end in cuts(ADDS):
            b = first // places
            picked = tables[b][:].indirect(offsets[:, (first - b * places) // 16 : (end - b * places) // 16])
            nc.vector.tensor_tensor(sums[:, first:end], picked, positions[:, first:end], ADD)
            for store_first, store_end in cuts(STORES):
                if store_end == end:
                    nc.sync.dma_start(out_rows[:, store_first:store_end], sums[:, store_first:store_end])
